import numpy as np
import ml_dtypes


def mxq(x, axis, fmt="e4m3"):
    dtype, down = {"e4m3": (ml_dtypes.float8_e4m3fn, 7), "e5m2": (ml_dtypes.float8_e5m2, 14)}[fmt]
    v = np.moveaxis(np.asarray(x, np.float32).astype(ml_dtypes.bfloat16).astype(np.float64), axis, -1)
    blocks = v.reshape(v.shape[:-1] + (-1, 32))
    amax = np.abs(blocks).max(-1, keepdims=True)
    byte = np.maximum(np.where(amax > 0, np.frexp(amax)[1] - 1 + 127, 0) - down, 1)
    scale = np.exp2(byte - 127.0)
    codes = (blocks / scale).astype(np.float32).astype(dtype).astype(np.float64)
    return np.moveaxis((codes * scale).reshape(v.shape), -1, axis)


WIDE = False


def mx_kscale(k):
    if not WIDE:
        return np.ones(k)
    levels = np.array([10, -10, 5, -5, 0])
    if k % 512:
        return np.exp2(np.random.permutation(np.resize(levels, k // 32))).repeat(32)
    a = np.empty((k // 512, 16))
    for p in range(k // 512):
        a[p, :8] = np.random.permutation(np.resize(levels, 8))
        for g in range(8):
            far = levels[np.abs(levels - a[p, g]) >= 10]
            a[p, g + 8] = far[np.random.randint(len(far))]
    return np.exp2(a.ravel()).repeat(32)


BF16 = ml_dtypes.bfloat16


def bf(x):
    return np.asarray(x, np.float32).astype(BF16)


def f64(x):
    return np.asarray(x).astype(np.float64)


B, C, Q, O, H, W = 2, 2560, 512, 512, 16, 32
N = H * W
SIG = 1.75


def setup_inputs():
    s = mx_kscale(N).reshape(H, W)
    return {"x": bf(np.random.standard_normal((B, C, H, W)) / s),
            "query": bf(np.random.standard_normal((B, Q, H, W)) * SIG / np.sqrt(N) * s)}


def core(x, query):
    xf = f64(x).reshape(B, C, N)
    qf = f64(query).reshape(B, Q, N)
    energy = mxq(qf, 2, "e4m3") @ mxq(xf, 2, "e4m3").transpose(0, 2, 1)
    energy_new = energy.max(-1, keepdims=True) - energy
    e = np.exp(energy_new - energy_new.max(-1, keepdims=True))
    return e / e.sum(-1, keepdims=True)


def e4m3fn_bytes(y):
    return np.clip(np.asarray(y, np.float64), -448.0, 448.0).astype(np.float32).astype(ml_dtypes.float8_e4m3fn).view(np.uint8)


Y_SCALE = 250000.0


def reference(x, query):
    out = core(x, query)
    return out, e4m3fn_bytes(out * Y_SCALE)

@@ -1,0 +1,226 @@
+from contextlib import ExitStack
+
+import concourse.mybir as mybir
+from concourse.masks import make_identity
+
+F32 = mybir.dt.float32
+BF16 = mybir.dt.bfloat16
+U32 = mybir.dt.uint32
+U8 = mybir.dt.uint8
+FP8X4 = mybir.dt.float8_e4m3fn_x4
+FP8 = mybir.dt.float8_e4m3fn
+ALU = mybir.AluOpType
+ACT = mybir.ActivationFunctionType
+AX = mybir.AxisListType
+
+B, C, Q, K = 2, 2560, 512, 512
+P = 128
+CHUNK = 512
+HALF = CHUNK // 2
+NCH = C // CHUNK
+QT = Q // P
+NJOB = B * QT
+Y_SCALE = 250000.0
+FLOPS = 2 * B * Q * C * K
+
+PT_BUFS = 3
+PS_BUFS = 5
+HEAD_EV = 3
+EV_PER_STEP = {0: 4, 1: 4, 2: 2}
+FILL_V = {7: [(1, 0, 2560)]}
+FILL_S = {3: [(0, 0, 512)], 4: [(0, 512, 1024)], 5: [(0, 1024, 1536)], 6: [(0, 1536, 2048)]}
+FIN = [(2048, 2048, 2560), (0, 0, 0), (0, 1152, 2560), (0, 1152, 2560), (0, 1152, 2560), (0, 1152, 2560), (0, 1280, 2560), (0, 1280, 2560)]
+C_ON_V = (7,)
+
+
+def tile_guided_cam_module_pa_kernel(tc, x, query, out_0, out_1):
+    nc = tc.nc
+    xv = x.rearrange("b (g h p l) y w -> b g p h (l y w)", g=NCH, h=2, p=P, l=2)
+    qv = query.rearrange("b (h p l) y w -> b p h (l y w)", h=2, p=P, l=2)
+
+    with ExitStack() as ctx:
+        ctx.enter_context(tc.manual_schedule())
+        const = ctx.enter_context(tc.tile_pool(name="const", bufs=1))
+        rawp = ctx.enter_context(tc.tile_pool(name="rawp", bufs=1))
+        keep = ctx.enter_context(tc.tile_pool(name="keep", bufs=1))
+        stage = ctx.enter_context(tc.tile_pool(name="stage", bufs=4))
+        work = ctx.enter_context(tc.tile_pool(name="work", bufs=1))
+        small = ctx.enter_context(tc.tile_pool(name="small", bufs=1))
+        psum_t = ctx.enter_context(tc.psum_pool(name="psum_t", bufs=PT_BUFS))
+        psum_e = ctx.enter_context(tc.psum_pool(name="psum_e", bufs=PS_BUFS))
+
+        halves = [(0, -1, 0)]
+        halves.extend([(0, g, h) for g in range(NCH) for h in range(2)])
+        halves.append((0, -1, 1))
+        halves.extend([(1, c, h) for c in range(-1, NCH) for h in range(2)])
+
+        raw = {}
+        for b in range(B):
+            for c in range(-1, NCH):
+                raw[(b, c)] = rawp.tile([P, 4 * K], BF16, name="raw_%d_%d" % (b, c + 1))
+
+        def load(b, c, h0, h1):
+            src = qv[b] if c < 0 else xv[b, c]
+            dst = raw[(b, c)][:].rearrange("p (h m) -> p h m", h=2)
+            nc.sync.dma_start(out=dst[:, h0:h1, :], in_=src[:, h0:h1, :])
+
+        load(0, -1, 0, 1)
+        for g in range(NCH):
+            load(0, g, 0, 2)
+        load(0, -1, 1, 2)
+        for c in range(-1, NCH):
+            load(1, c, 0, 2)
+
+        ident = const.tile([P, P], F32, name="ident")
+        make_identity(nc, ident[:])
+        warm = const.tile([P, 2], F32, name="warm")
+        nc.vector.memset(warm[:], 0.0)
+        nc.scalar.activation(out=warm[:, 1:2], in_=warm[:, 0:1], func=ACT.Exp)
+
+        qc = [keep.tile([P, Q], U32, name="qc%d" % b, align_bytes=64) for b in range(B)]
+        qs = [keep.tile([P, Q], U8, name="qs%d" % b, align_bytes=64) for b in range(B)]
+        xc = [keep.tile([P, C], U32, name="xc%d" % b, align_bytes=64) for b in range(B)]
+        xs = [keep.tile([P, C], U8, name="xs%d" % b, align_bytes=64) for b in range(B)]
+        W = [work.tile([P, C], F32, name="W%d" % j) for j in range(NJOB)]
+        f8 = [work.tile([P, C], FP8, name="f8_%d" % j) for j in range(NJOB)]
+        mins = [small.tile([P, NCH], F32, name="mins%d" % j) for j in range(NJOB)]
+        rmin = [small.tile([P, 1], F32, name="rmin%d" % j) for j in range(NJOB)]
+        ssum = [small.tile([P, 1], F32, name="ssum%d" % j) for j in range(NJOB)]
+        rinv = [small.tile([P, 1], F32, name="rinv%d" % j) for j in range(NJOB)]
+
+        st = {"nt": 0, "ne": 0, "pend": []}
+
+        def tp_next():
+            k = st["nt"]
+            if k >= len(halves):
+                return
+            b, c, h = halves[k]
+            words = raw[(b, c)][:].bitcast(F32)
+            pt = psum_t.tile([P, 4, P], F32, name="pt", tag="pt")
+            for l in range(2):
+                for u in range(2):
+                    s = 2 * h + l
+                    nc.tensor.transpose(pt[:, 2 * l + u, :], words[:, s * 256 + u : (s + 1) * 256 : 2], ident[:])
+            st[("pt", k)] = pt
+            st["nt"] = k + 1
+
+        def ev_next():
+            k = st["ne"]
+            b, c, h = halves[k]
+            alone = b == 0 and c < 0
+            if alone or h == 0:
+                st[("grp", b, c)] = stage.tile([P, 4 * CHUNK], BF16, name="grp", tag="grp", align_bytes=64)
+            grp = st[("grp", b, c)]
+            pos = 0 if alone else h
+            dst = grp[:].bitcast(F32)[:, 512 * pos : 512 * (pos + 1)].rearrange("k (p a) -> k p a", a=4)
+            nc.scalar.copy(out=dst, in_=st[("pt", k)][:].rearrange("k a p -> k p a"))
+            if alone:
+                st["pend"].append((b, c, h, 1))
+            elif h == 1:
+                st["pend"].append((b, c, 0, 2))
+            st["ne"] = k + 1
+
+        def flush_q():
+            for b, c, h, n in st["pend"]:
+                grp = st[("grp", b, c)]
+                lo = (0 if c < 0 else c * CHUNK) + h * HALF
+                codes, scales = (qc[b], qs[b]) if c < 0 else (xc[b], xs[b])
+                nc.vector.quantize_mx(
+                    out=codes[:, lo : lo + n * HALF].bitcast(FP8X4),
+                    scales=scales[:, lo : lo + n * HALF],
+                    in_=grp[:, 0 : n * 4 * HALF],
+                )
+            st["pend"] = []
+
+        def energy(j, g):
+            b, i = divmod(j, QT)
+            ps = psum_e.tile([P, CHUNK], F32, name="ps", tag="ps")
+            nc.tensor.matmul_mx(
+                out=ps[:],
+                lhsT=qc[b][:, i * P : (i + 1) * P].bitcast(FP8X4),
+                lhsT_scale=qs[b][:, i * P : (i + 1) * P],
+                rhs=xc[b][:, g * CHUNK : (g + 1) * CHUNK].bitcast(FP8X4),
+                rhs_scale=xs[b][:, g * CHUNK : (g + 1) * CHUNK],
+                start=True,
+                stop=True,
+            )
+            nc.vector.tensor_scalar(
+                out=W[j][:, g * CHUNK : (g + 1) * CHUNK],
+                in0=ps[:],
+                scalar1=1.0,
+                scalar2=None,
+                op0=ALU.mult,
+                op1=ALU.min,
+                accum_out=mins[j][:, g : g + 1],
+            )
+
+        def rowmin(j):
+            nc.vector.tensor_reduce(out=rmin[j][:], in_=mins[j][:], axis=AX.X, op=ALU.min)
+
+        def expo(j):
+            nc.scalar.activation(out=W[j][:], in_=W[j][:], func=ACT.Exp, bias=rmin[j][:, 0:1], scale=-1.0, accum_out=ssum[j][:, 0:1])
+
+        def norm(j):
+            b, i = divmod(j, QT)
+            nc.vector.reciprocal(out=rinv[j][:], in_=ssum[j][:])
+            for g in range(NCH):
+                sl = slice(g * CHUNK, (g + 1) * CHUNK)
+                if j in C_ON_V:
+                    nc.vector.tensor_scalar(out=W[j][:, sl], in0=W[j][:, sl], scalar1=rinv[j][:, 0:1], scalar2=None, op0=ALU.mult)
+                else:
+                    nc.gpsimd.tensor_scalar(out=W[j][:, sl], in0=W[j][:, sl], scalar1=rinv[j][:, 0:1], scalar2=0.0, op0=ALU.mult, op1=ALU.add)
+                nc.sync.dma_start(out=out_0[b, i * P : (i + 1) * P, sl], in_=W[j][:, sl])
+
+        def cast_s(j, lo, hi):
+            if hi > lo:
+                nc.scalar.activation(out=f8[j][:, lo:hi], in_=W[j][:, lo:hi], func=ACT.Copy, scale=Y_SCALE, saturate=False)
+
+        def cast_v(j, lo, hi):
+            if hi > lo:
+                tmp = work.tile([P, C], F32, name="tmp", tag="tmp", bufs=2)
+                nc.vector.tensor_scalar(out=tmp[:, 0 : hi - lo], in0=W[j][:, lo:hi], scalar1=Y_SCALE, scalar2=None, op0=ALU.mult)
+                nc.vector.tensor_copy(out=f8[j][:, lo:hi], in_=tmp[:, 0 : hi - lo], saturate=False)
+
+        def store_bytes(j):
+            b, i = divmod(j, QT)
+            nc.sync.dma_start(out=out_1[b, i * P : (i + 1) * P, :], in_=f8[j][:].bitcast(U8))
+
+        for k in range(PT_BUFS):
+            tp_next()
+        for k in range(2 * NCH + 1):
+            ev_next()
+            c = halves[k][1]
+            full = len(st["pend"]) > 0
+            flush_q()
+            if full and c >= 1:
+                energy(0, c - 1)
+            if k == 2 * NCH:
+                energy(0, NCH - 1)
+            tp_next()
+        rowmin(0)
+        for k in range(HEAD_EV):
+            ev_next()
+
+        for j in range(NJOB):
+            expo(j)
+            flush_q()
+            if j + 1 < NJOB:
+                for g in range(NCH):
+                    energy(j + 1, g)
+                rowmin(j + 1)
+            while st["nt"] < min(len(halves), st["ne"] + PT_BUFS):
+                tp_next()
+            for jj, lo, hi in FILL_V.get(j, []):
+                cast_v(jj, lo, hi)
+            norm(j)
+            for k in range(EV_PER_STEP.get(j, 0)):
+                ev_next()
+                tp_next()
+            for jj, lo, hi in FILL_S.get(j, []):
+                cast_s(jj, lo, hi)
+
+        for j in range(NJOB):
+            lo, mid, hi = FIN[j]
+            cast_s(j, mid, hi)
+            cast_v(j, lo, mid)
+            store_bytes(j)

@@ -24,6 +24,7 @@ Y_SCALE = 250000.0
 FLOPS = 2 * B * Q * C * K
 
 PT_BUFS = 3
+WARM_START = 6
 PS_BUFS = 5
 HEAD_EV = 3
 EV_PER_STEP = {0: 4, 1: 4, 2: 2}
@@ -70,6 +71,16 @@ def tile_guided_cam_module_pa_kernel(tc, x, query, out_0, out_1):
         load(0, -1, 1, 2)
         for c in range(-1, NCH):
             load(1, c, 0, 2)
+
+        zt = const.tile([P, CHUNK], BF16, name="zt")
+        nc.vector.memset(zt[:], 0.0)
+
+        def dummy():
+            ps = psum_e.tile([P, CHUNK], F32, name="ps", tag="ps")
+            nc.tensor.matmul(out=ps[:], lhsT=zt[:, 0:P], rhs=zt[:], start=True, stop=True)
+
+        for k in range(WARM_START):
+            dummy()
 
         ident = const.tile([P, P], F32, name="ident")
         make_identity(nc, ident[:])
@@ -187,6 +198,8 @@ def tile_guided_cam_module_pa_kernel(tc, x, query, out_0, out_1):
 
         for k in range(PT_BUFS):
             tp_next()
+            if k % 2 == 0:
+                dummy()
         for k in range(2 * NCH + 1):
             ev_next()
             c = halves[k][1]
@@ -197,6 +210,8 @@ def tile_guided_cam_module_pa_kernel(tc, x, query, out_0, out_1):
             if k == 2 * NCH:
                 energy(0, NCH - 1)
             tp_next()
+            if k in (1, 3):
+                dummy()
         rowmin(0)
         for k in range(HEAD_EV):
             ev_next()

@@ -28,16 +28,20 @@ WARM_START = 6
 PS_BUFS = 5
 HEAD_EV = 3
 EV_PER_STEP = {0: 4, 1: 4, 2: 2}
-FILL_V = {7: [(1, 0, 2560)]}
-FILL_S = {3: [(0, 0, 512)], 4: [(0, 512, 1024)], 5: [(0, 1024, 1536)], 6: [(0, 1536, 2048)]}
-FIN = [(2048, 2048, 2560), (0, 0, 0), (0, 1152, 2560), (0, 1152, 2560), (0, 1152, 2560), (0, 1152, 2560), (0, 1280, 2560), (0, 1280, 2560)]
-C_ON_V = (7,)
+LAST_PREP_STEP = 2
+FILL_V = {7: [(2, 0, 768)]}
+FILL_S = {2: [(0, 0, 512)], 3: [(0, 512, 1280)], 4: [(0, 1280, 2304)], 5: [(0, 2304, 2560), (1, 0, 512)], 6: [(1, 512, 1024)]}
+FIN = [(2560, 2560, 2560), (1024, 1664, 2560), (768, 1536, 2560), (0, 1024, 2560), (0, 1024, 2560), (0, 1024, 2560), (0, 1024, 2560), (0, 1024, 2560)]
+C_ON_V = (6, 7)
+C_PIECES = 2
 
 
 def tile_guided_cam_module_pa_kernel(tc, x, query, out_0, out_1):
     nc = tc.nc
     xv = x.rearrange("b (g h p l) y w -> b g p h (l y w)", g=NCH, h=2, p=P, l=2)
     qv = query.rearrange("b (h p l) y w -> b p h (l y w)", h=2, p=P, l=2)
+    o0v = out_0.rearrange("b (i p l) c -> b i l p c", i=2, p=P, l=2)
+    o1v = out_1.rearrange("b (i p l) c -> b i l p c", i=2, p=P, l=2)
 
     with ExitStack() as ctx:
         ctx.enter_context(tc.manual_schedule())
@@ -123,8 +127,8 @@ def tile_guided_cam_module_pa_kernel(tc, x, query, out_0, out_1):
                 st[("grp", b, c)] = stage.tile([P, 4 * CHUNK], BF16, name="grp", tag="grp", align_bytes=64)
             grp = st[("grp", b, c)]
             pos = 0 if alone else h
-            dst = grp[:].bitcast(F32)[:, 512 * pos : 512 * (pos + 1)].rearrange("k (p a) -> k p a", a=4)
-            nc.scalar.copy(out=dst, in_=st[("pt", k)][:].rearrange("k a p -> k p a"))
+            dst = grp[:].bitcast(F32)[:, 512 * pos : 512 * (pos + 1)].rearrange("k (l p u) -> k l p u", l=2, u=2)
+            nc.scalar.copy(out=dst, in_=st[("pt", k)][:].rearrange("k (l u) p -> k l p u", l=2))
             if alone:
                 st["pend"].append((b, c, h, 1))
             elif h == 1:
@@ -143,7 +147,7 @@ def tile_guided_cam_module_pa_kernel(tc, x, query, out_0, out_1):
                 )
             st["pend"] = []
 
-        def energy(j, g):
+        def mm(j, g):
             b, i = divmod(j, QT)
             ps = psum_e.tile([P, CHUNK], F32, name="ps", tag="ps")
             nc.tensor.matmul_mx(
@@ -155,9 +159,12 @@ def tile_guided_cam_module_pa_kernel(tc, x, query, out_0, out_1):
                 start=True,
                 stop=True,
             )
+            st[("ps", j, g)] = ps
+
+        def take(j, g):
             nc.vector.tensor_scalar(
-                out=W[j][:, g * CHUNK : (g + 1) * CHUNK],
-                in0=ps[:],
+                out=W[j][:, g * CHUNK : (g + 1) * CHUNK].rearrange("q (h p l) -> q h p l", h=2, l=2),
+                in0=st[("ps", j, g)][:].rearrange("q (h l p) -> q h p l", h=2, l=2),
                 scalar1=1.0,
                 scalar2=None,
                 op0=ALU.mult,
@@ -174,27 +181,30 @@ def tile_guided_cam_module_pa_kernel(tc, x, query, out_0, out_1):
         def norm(j):
             b, i = divmod(j, QT)
             nc.vector.reciprocal(out=rinv[j][:], in_=ssum[j][:])
-            for g in range(NCH):
-                sl = slice(g * CHUNK, (g + 1) * CHUNK)
+            wd = C // C_PIECES
+            for g in range(C_PIECES):
+                sl = slice(g * wd, (g + 1) * wd)
                 if j in C_ON_V:
                     nc.vector.tensor_scalar(out=W[j][:, sl], in0=W[j][:, sl], scalar1=rinv[j][:, 0:1], scalar2=None, op0=ALU.mult)
                 else:
                     nc.gpsimd.tensor_scalar(out=W[j][:, sl], in0=W[j][:, sl], scalar1=rinv[j][:, 0:1], scalar2=0.0, op0=ALU.mult, op1=ALU.add)
-                nc.sync.dma_start(out=out_0[b, i * P : (i + 1) * P, sl], in_=W[j][:, sl])
+                nc.sync.dma_start(out=o0v[b, i // 2, i % 2, :, sl], in_=W[j][:, sl])
 
         def cast_s(j, lo, hi):
             if hi > lo:
                 nc.scalar.activation(out=f8[j][:, lo:hi], in_=W[j][:, lo:hi], func=ACT.Copy, scale=Y_SCALE, saturate=False)
 
-        def cast_v(j, lo, hi):
-            if hi > lo:
-                tmp = work.tile([P, C], F32, name="tmp", tag="tmp", bufs=2)
-                nc.vector.tensor_scalar(out=tmp[:, 0 : hi - lo], in0=W[j][:, lo:hi], scalar1=Y_SCALE, scalar2=None, op0=ALU.mult)
-                nc.vector.tensor_copy(out=f8[j][:, lo:hi], in_=tmp[:, 0 : hi - lo], saturate=False)
+        def scale_v(j, lo, hi):
+            tmp = work.tile([P, C // 2], F32, name="tmp", tag="tmp", bufs=3)
+            nc.vector.tensor_scalar(out=tmp[:, 0 : hi - lo], in0=W[j][:, lo:hi], scalar1=Y_SCALE, scalar2=None, op0=ALU.mult)
+            return tmp
+
+        def cast_v(j, lo, hi, tmp):
+            nc.vector.tensor_copy(out=f8[j][:, lo:hi], in_=tmp[:, 0 : hi - lo], saturate=False)
 
         def store_bytes(j):
             b, i = divmod(j, QT)
-            nc.sync.dma_start(out=out_1[b, i * P : (i + 1) * P, :], in_=f8[j][:].bitcast(U8))
+            nc.sync.dma_start(out=o1v[b, i // 2, i % 2], in_=f8[j][:].bitcast(U8))
 
         for k in range(PT_BUFS):
             tp_next()
@@ -206,36 +216,60 @@ def tile_guided_cam_module_pa_kernel(tc, x, query, out_0, out_1):
             full = len(st["pend"]) > 0
             flush_q()
             if full and c >= 1:
-                energy(0, c - 1)
+                mm(0, c - 1)
+                take(0, c - 1)
             if k == 2 * NCH:
-                energy(0, NCH - 1)
+                mm(0, NCH - 1)
+                take(0, NCH - 1)
             tp_next()
             if k in (1, 3):
                 dummy()
         rowmin(0)
+        for g in range(NCH):
+            mm(1, g)
         for k in range(HEAD_EV):
             ev_next()
 
         for j in range(NJOB):
             expo(j)
-            flush_q()
             if j + 1 < NJOB:
                 for g in range(NCH):
-                    energy(j + 1, g)
+                    take(j + 1, g)
                 rowmin(j + 1)
+            flush_q()
             while st["nt"] < min(len(halves), st["ne"] + PT_BUFS):
                 tp_next()
-            for jj, lo, hi in FILL_V.get(j, []):
-                cast_v(jj, lo, hi)
-            norm(j)
+            if j + 2 < NJOB and j != LAST_PREP_STEP:
+                for g in range(NCH):
+                    mm(j + 2, g)
             for k in range(EV_PER_STEP.get(j, 0)):
                 ev_next()
                 tp_next()
+            if j == LAST_PREP_STEP:
+                flush_q()
+                for g in range(NCH):
+                    mm(j + 2, g)
+            for jj, lo, hi in FILL_V.get(j, []):
+                mid = (lo + hi) // 2
+                t0 = scale_v(jj, lo, mid)
+                t1 = scale_v(jj, mid, hi)
+                cast_v(jj, lo, mid, t0)
+                cast_v(jj, mid, hi, t1)
+            norm(j)
             for jj, lo, hi in FILL_S.get(j, []):
                 cast_s(jj, lo, hi)
 
+        prev = None
         for j in range(NJOB):
             lo, mid, hi = FIN[j]
             cast_s(j, mid, hi)
-            cast_v(j, lo, mid)
-            store_bytes(j)
+            cur = (j, lo, mid, scale_v(j, lo, mid)) if mid > lo else None
+            if prev is not None:
+                cast_v(prev[0], prev[1], prev[2], prev[3])
+                store_bytes(prev[0])
+            if cur is None:
+                store_bytes(j)
+            prev = cur
+        if prev is not None:
+            cast_v(prev[0], prev[1], prev[2], prev[3])
+            store_bytes(prev[0])

@@ -31,9 +31,10 @@ EV_PER_STEP = {0: 4, 1: 4, 2: 2}
 LAST_PREP_STEP = 2
 FILL_V = {7: [(2, 0, 768)]}
 FILL_S = {2: [(0, 0, 512)], 3: [(0, 512, 1280)], 4: [(0, 1280, 2304)], 5: [(0, 2304, 2560), (1, 0, 512)], 6: [(1, 512, 1024)]}
-FIN = [(2560, 2560, 2560), (1024, 1664, 2560), (768, 1536, 2560), (0, 1024, 2560), (0, 1024, 2560), (0, 1024, 2560), (0, 1024, 2560), (0, 1024, 2560)]
+FIN = [(2560, 2560, 2560), (1024, 1664, 2560), (768, 1536, 2560), (0, 1280, 2560), (0, 1280, 2560), (0, 1280, 2560), (0, 1280, 2560), (0, 1280, 2560)]
 C_ON_V = (6, 7)
 C_PIECES = 2
+SPLIT_LAST = 2
 
 
 def tile_guided_cam_module_pa_kernel(tc, x, query, out_0, out_1):
@@ -202,9 +203,10 @@ def tile_guided_cam_module_pa_kernel(tc, x, query, out_0, out_1):
         def cast_v(j, lo, hi, tmp):
             nc.vector.tensor_copy(out=f8[j][:, lo:hi], in_=tmp[:, 0 : hi - lo], saturate=False)
 
-        def store_bytes(j):
+        def store_bytes(j, lo, hi):
             b, i = divmod(j, QT)
-            nc.sync.dma_start(out=o1v[b, i // 2, i % 2], in_=f8[j][:].bitcast(U8))
+            if hi > lo:
+                nc.sync.dma_start(out=o1v[b, i // 2, i % 2, :, lo:hi], in_=f8[j][:, lo:hi].bitcast(U8))
 
         for k in range(PT_BUFS):
             tp_next()
@@ -232,9 +234,12 @@ def tile_guided_cam_module_pa_kernel(tc, x, query, out_0, out_1):
 
         for j in range(NJOB):
             expo(j)
+            early = j > LAST_PREP_STEP and j not in C_ON_V
             if j + 1 < NJOB:
                 for g in range(NCH):
                     take(j + 1, g)
+                if early:
+                    norm(j)
                 rowmin(j + 1)
             flush_q()
             while st["nt"] < min(len(halves), st["ne"] + PT_BUFS):
@@ -255,7 +260,8 @@ def tile_guided_cam_module_pa_kernel(tc, x, query, out_0, out_1):
                 t1 = scale_v(jj, mid, hi)
                 cast_v(jj, lo, mid, t0)
                 cast_v(jj, mid, hi, t1)
-            norm(j)
+            if not early:
+                norm(j)
             for jj, lo, hi in FILL_S.get(j, []):
                 cast_s(jj, lo, hi)
 
@@ -263,13 +269,16 @@ def tile_guided_cam_module_pa_kernel(tc, x, query, out_0, out_1):
         for j in range(NJOB):
             lo, mid, hi = FIN[j]
             cast_s(j, mid, hi)
-            cur = (j, lo, mid, scale_v(j, lo, mid)) if mid > lo else None
+            split = j >= NJOB - SPLIT_LAST
+            if split:
+                store_bytes(j, mid, C)
+            cur = (j, lo, mid, scale_v(j, lo, mid), split) if mid > lo else None
             if prev is not None:
                 cast_v(prev[0], prev[1], prev[2], prev[3])
-                store_bytes(prev[0])
+                store_bytes(prev[0], 0, prev[2] if prev[4] else C)
             if cur is None:
-                store_bytes(j)
+                store_bytes(j, 0, mid if split else C)
             prev = cur
         if prev is not None:
             cast_v(prev[0], prev[1], prev[2], prev[3])
-            store_bytes(prev[0])
+            store_bytes(prev[0], 0, prev[2] if prev[4] else C)

@@ -31,7 +31,7 @@ EV_PER_STEP = {0: 4, 1: 4, 2: 2}
 LAST_PREP_STEP = 2
 FILL_V = {7: [(2, 0, 768)]}
 FILL_S = {2: [(0, 0, 512)], 3: [(0, 512, 1280)], 4: [(0, 1280, 2304)], 5: [(0, 2304, 2560), (1, 0, 512)], 6: [(1, 512, 1024)]}
-FIN = [(2560, 2560, 2560), (1024, 1664, 2560), (768, 1536, 2560), (0, 1280, 2560), (0, 1280, 2560), (0, 1280, 2560), (0, 1280, 2560), (0, 1280, 2560)]
+FIN = [(2560, 2560, 2560), (1024, 1664, 2560), (768, 1536, 2560), (0, 1152, 2560), (0, 1152, 2560), (0, 1152, 2560), (0, 1152, 2560), (0, 1152, 2560)]
 C_ON_V = (6, 7)
 C_PIECES = 2
 SPLIT_LAST = 2

@@ -29,12 +29,11 @@ PS_BUFS = 5
 HEAD_EV = 3
 EV_PER_STEP = {0: 4, 1: 4, 2: 2}
 LAST_PREP_STEP = 2
-FILL_V = {7: [(2, 0, 768)]}
-FILL_S = {2: [(0, 0, 512)], 3: [(0, 512, 1280)], 4: [(0, 1280, 2304)], 5: [(0, 2304, 2560), (1, 0, 512)], 6: [(1, 512, 1024)]}
-FIN = [(2560, 2560, 2560), (1024, 1664, 2560), (768, 1536, 2560), (0, 1152, 2560), (0, 1152, 2560), (0, 1152, 2560), (0, 1152, 2560), (0, 1152, 2560)]
+FILL_V = {1: [(0, 0, 1280)], 2: [(0, 1280, 2560)], 7: [(1, 0, 1280), (1, 1280, 2560)]}
+FIRST_END_JOB = 2
+V_SHARE = 1536
 C_ON_V = (6, 7)
 C_PIECES = 2
-SPLIT_LAST = 2
 
 
 def tile_guided_cam_module_pa_kernel(tc, x, query, out_0, out_1):
@@ -195,13 +194,8 @@ def tile_guided_cam_module_pa_kernel(tc, x, query, out_0, out_1):
             if hi > lo:
                 nc.scalar.activation(out=f8[j][:, lo:hi], in_=W[j][:, lo:hi], func=ACT.Copy, scale=Y_SCALE, saturate=False)
 
-        def scale_v(j, lo, hi):
-            tmp = work.tile([P, C // 2], F32, name="tmp", tag="tmp", bufs=3)
-            nc.vector.tensor_scalar(out=tmp[:, 0 : hi - lo], in0=W[j][:, lo:hi], scalar1=Y_SCALE, scalar2=None, op0=ALU.mult)
-            return tmp
-
-        def cast_v(j, lo, hi, tmp):
-            nc.vector.tensor_copy(out=f8[j][:, lo:hi], in_=tmp[:, 0 : hi - lo], saturate=False)
+        def cast_v(j, lo, hi):
+            nc.vector.tensor_scalar(out=f8[j][:, lo:hi], in0=W[j][:, lo:hi], scalar1=Y_SCALE, scalar2=None, op0=ALU.mult, saturate=False)
 
         def store_bytes(j, lo, hi):
             b, i = divmod(j, QT)
@@ -255,30 +249,13 @@ def tile_guided_cam_module_pa_kernel(tc, x, query, out_0, out_1):
                 for g in range(NCH):
                     mm(j + 2, g)
             for jj, lo, hi in FILL_V.get(j, []):
-                mid = (lo + hi) // 2
-                t0 = scale_v(jj, lo, mid)
-                t1 = scale_v(jj, mid, hi)
-                cast_v(jj, lo, mid, t0)
-                cast_v(jj, mid, hi, t1)
+                cast_v(jj, lo, hi)
+                store_bytes(jj, lo, hi)
             if not early:
                 norm(j)
-            for jj, lo, hi in FILL_S.get(j, []):
-                cast_s(jj, lo, hi)
 
-        prev = None
-        for j in range(NJOB):
-            lo, mid, hi = FIN[j]
-            cast_s(j, mid, hi)
-            split = j >= NJOB - SPLIT_LAST
-            if split:
-                store_bytes(j, mid, C)
-            cur = (j, lo, mid, scale_v(j, lo, mid), split) if mid > lo else None
-            if prev is not None:
-                cast_v(prev[0], prev[1], prev[2], prev[3])
-                store_bytes(prev[0], 0, prev[2] if prev[4] else C)
-            if cur is None:
-                store_bytes(j, 0, mid if split else C)
-            prev = cur
-        if prev is not None:
-            cast_v(prev[0], prev[1], prev[2], prev[3])
-            store_bytes(prev[0], 0, prev[2] if prev[4] else C)
+        for j in range(FIRST_END_JOB, NJOB):
+            cast_v(j, 0, V_SHARE)
+            store_bytes(j, 0, V_SHARE)
+            cast_s(j, V_SHARE, C)
+            store_bytes(j, V_SHARE, C)

@@ -29,11 +29,8 @@ PS_BUFS = 5
 HEAD_EV = 3
 EV_PER_STEP = {0: 4, 1: 4, 2: 2}
 LAST_PREP_STEP = 2
-FILL_V = {1: [(0, 0, 1280)], 2: [(0, 1280, 2560)], 7: [(1, 0, 1280), (1, 1280, 2560)]}
-FIRST_END_JOB = 2
-V_SHARE = 1536
 C_ON_V = (6, 7)
-C_PIECES = 2
+HC = C // 2
 
 
 def tile_guided_cam_module_pa_kernel(tc, x, query, out_0, out_1):
@@ -178,12 +175,11 @@ def tile_guided_cam_module_pa_kernel(tc, x, query, out_0, out_1):
         def expo(j):
             nc.scalar.activation(out=W[j][:], in_=W[j][:], func=ACT.Exp, bias=rmin[j][:, 0:1], scale=-1.0, accum_out=ssum[j][:, 0:1])
 
-        def norm(j):
+        def norm(j, order=(0, 1)):
             b, i = divmod(j, QT)
             nc.vector.reciprocal(out=rinv[j][:], in_=ssum[j][:])
-            wd = C // C_PIECES
-            for g in range(C_PIECES):
-                sl = slice(g * wd, (g + 1) * wd)
+            for g in order:
+                sl = slice(g * HC, (g + 1) * HC)
                 if j in C_ON_V:
                     nc.vector.tensor_scalar(out=W[j][:, sl], in0=W[j][:, sl], scalar1=rinv[j][:, 0:1], scalar2=None, op0=ALU.mult)
                 else:
@@ -226,15 +222,13 @@ def tile_guided_cam_module_pa_kernel(tc, x, query, out_0, out_1):
         for k in range(HEAD_EV):
             ev_next()
 
-        for j in range(NJOB):
+        for j in range(NJOB - 1):
             expo(j)
-            early = j > LAST_PREP_STEP and j not in C_ON_V
-            if j + 1 < NJOB:
-                for g in range(NCH):
-                    take(j + 1, g)
-                if early:
-                    norm(j)
-                rowmin(j + 1)
+            for g in range(NCH):
+                take(j + 1, g)
+            rowmin(j + 1)
+            if j >= 1:
+                cast_v(j - 1, 0, HC)
             flush_q()
             while st["nt"] < min(len(halves), st["ne"] + PT_BUFS):
                 tp_next()
@@ -248,14 +242,20 @@ def tile_guided_cam_module_pa_kernel(tc, x, query, out_0, out_1):
                 flush_q()
                 for g in range(NCH):
                     mm(j + 2, g)
-            for jj, lo, hi in FILL_V.get(j, []):
-                cast_v(jj, lo, hi)
-                store_bytes(jj, lo, hi)
-            if not early:
-                norm(j)
+            if j >= 2:
+                cast_s(j - 2, HC, C)
+                store_bytes(j - 2, 0, C)
+            norm(j)
 
-        for j in range(FIRST_END_JOB, NJOB):
-            cast_v(j, 0, V_SHARE)
-            store_bytes(j, 0, V_SHARE)
-            cast_s(j, V_SHARE, C)
-            store_bytes(j, V_SHARE, C)
+        last = NJOB - 1
+        expo(last)
+        cast_v(last - 1, 0, HC)
+        cast_s(last - 2, HC, C)
+        store_bytes(last - 2, 0, C)
+        norm(last, (1, 0))
+        cast_v(last - 1, HC, C)
+        store_bytes(last - 1, 0, C)
+        cast_s(last, HC, C)
+        store_bytes(last, HC, C)
+        cast_v(last, 0, HC)
+        store_bytes(last, 0, HC)

@@ -35,7 +35,7 @@ HC = C // 2
 
 def tile_guided_cam_module_pa_kernel(tc, x, query, out_0, out_1):
     nc = tc.nc
-    xv = x.rearrange("b (g h p l) y w -> b g p h (l y w)", g=NCH, h=2, p=P, l=2)
+    xv = x.rearrange("b (g p s) y w -> b g p (s y w)", g=NCH, p=P, s=4)
     qv = query.rearrange("b (h p l) y w -> b p h (l y w)", h=2, p=P, l=2)
     o0v = out_0.rearrange("b (i p l) c -> b i l p c", i=2, p=P, l=2)
     o1v = out_1.rearrange("b (i p l) c -> b i l p c", i=2, p=P, l=2)
@@ -62,9 +62,11 @@ def tile_guided_cam_module_pa_kernel(tc, x, query, out_0, out_1):
                 raw[(b, c)] = rawp.tile([P, 4 * K], BF16, name="raw_%d_%d" % (b, c + 1))
 
         def load(b, c, h0, h1):
-            src = qv[b] if c < 0 else xv[b, c]
-            dst = raw[(b, c)][:].rearrange("p (h m) -> p h m", h=2)
-            nc.sync.dma_start(out=dst[:, h0:h1, :], in_=src[:, h0:h1, :])
+            if c < 0:
+                dst = raw[(b, c)][:].rearrange("p (h m) -> p h m", h=2)
+                nc.sync.dma_start(out=dst[:, h0:h1, :], in_=qv[b][:, h0:h1, :])
+            else:
+                nc.sync.dma_start(out=raw[(b, c)][:], in_=xv[b, c])
 
         load(0, -1, 0, 1)
         for g in range(NCH):
@@ -160,8 +162,8 @@ def tile_guided_cam_module_pa_kernel(tc, x, query, out_0, out_1):
 
         def take(j, g):
             nc.vector.tensor_scalar(
-                out=W[j][:, g * CHUNK : (g + 1) * CHUNK].rearrange("q (h p l) -> q h p l", h=2, l=2),
-                in0=st[("ps", j, g)][:].rearrange("q (h l p) -> q h p l", h=2, l=2),
+                out=W[j][:, g * CHUNK : (g + 1) * CHUNK].rearrange("q (p s) -> q p s", s=4),
+                in0=st[("ps", j, g)][:].rearrange("q (s p) -> q p s", s=4),
                 scalar1=1.0,
                 scalar2=None,
                 op0=ALU.mult,

@@ -223,6 +223,7 @@ def tile_guided_cam_module_pa_kernel(tc, x, query, out_0, out_1):
             mm(1, g)
         for k in range(HEAD_EV):
             ev_next()
+        flush_q()
 
         for j in range(NJOB - 1):
             expo(j)
@@ -244,19 +245,21 @@ def tile_guided_cam_module_pa_kernel(tc, x, query, out_0, out_1):
                 flush_q()
                 for g in range(NCH):
                     mm(j + 2, g)
+            if j in C_ON_V:
+                norm(j)
             if j >= 2:
                 cast_s(j - 2, HC, C)
                 store_bytes(j - 2, 0, C)
-            norm(j)
+            if j not in C_ON_V:
+                norm(j)
 
         last = NJOB - 1
         expo(last)
-        cast_v(last - 1, 0, HC)
-        cast_s(last - 2, HC, C)
+        cast_v(last - 2, HC, C)
         store_bytes(last - 2, 0, C)
-        norm(last, (1, 0))
-        cast_v(last - 1, HC, C)
+        cast_v(last - 1, 0, C)
         store_bytes(last - 1, 0, C)
+        norm(last, (1, 0))
         cast_s(last, HC, C)
         store_bytes(last, HC, C)
         cast_v(last, 0, HC)

@@ -232,6 +232,7 @@ def tile_guided_cam_module_pa_kernel(tc, x, query, out_0, out_1):
             rowmin(j + 1)
             if j >= 1:
                 cast_v(j - 1, 0, HC)
+                store_bytes(j - 1, 0, HC)
             flush_q()
             while st["nt"] < min(len(halves), st["ne"] + PT_BUFS):
                 tp_next()
@@ -249,14 +250,14 @@ def tile_guided_cam_module_pa_kernel(tc, x, query, out_0, out_1):
                 norm(j)
             if j >= 2:
                 cast_s(j - 2, HC, C)
-                store_bytes(j - 2, 0, C)
+                store_bytes(j - 2, HC, C)
             if j not in C_ON_V:
                 norm(j)
 
         last = NJOB - 1
         expo(last)
         cast_v(last - 2, HC, C)
-        store_bytes(last - 2, 0, C)
+        store_bytes(last - 2, HC, C)
         cast_v(last - 1, 0, C)
         store_bytes(last - 1, 0, C)
         norm(last, (1, 0))

@@ -27,7 +27,7 @@ PT_BUFS = 3
 WARM_START = 6
 PS_BUFS = 5
 HEAD_EV = 3
-EV_PER_STEP = {0: 4, 1: 4, 2: 2}
+EV_PER_STEP = {0: 3, 1: 4, 2: 3}
 LAST_PREP_STEP = 2
 C_ON_V = (6, 7)
 HC = C // 2

@@ -24,7 +24,7 @@ Y_SCALE = 250000.0
 FLOPS = 2 * B * Q * C * K
 
 PT_BUFS = 3
-WARM_START = 6
+WARM_START = 4
 PS_BUFS = 5
 HEAD_EV = 3
 EV_PER_STEP = {0: 3, 1: 4, 2: 3}
@@ -65,6 +65,9 @@ def tile_guided_cam_module_pa_kernel(tc, x, query, out_0, out_1):
             if c < 0:
                 dst = raw[(b, c)][:].rearrange("p (h m) -> p h m", h=2)
                 nc.sync.dma_start(out=dst[:, h0:h1, :], in_=qv[b][:, h0:h1, :])
+            elif b == 0 and c in (0,):
+                for h in range(2):
+                    nc.sync.dma_start(out=raw[(b, c)][:, h * 2 * K : (h + 1) * 2 * K], in_=xv[b, c][:, h * 2 * K : (h + 1) * 2 * K])
             else:
                 nc.sync.dma_start(out=raw[(b, c)][:], in_=xv[b, c])
 

from contextlib import ExitStack

import concourse.mybir as mybir
from concourse.masks import make_identity

F32 = mybir.dt.float32
BF16 = mybir.dt.bfloat16
U32 = mybir.dt.uint32
U8 = mybir.dt.uint8
FP8X4 = mybir.dt.float8_e4m3fn_x4
FP8 = mybir.dt.float8_e4m3fn
ALU = mybir.AluOpType
ACT = mybir.ActivationFunctionType
AX = mybir.AxisListType

B, C, Q, K = 2, 2560, 512, 512
P = 128
CHUNK = 512
HALF = CHUNK // 2
NCH = C // CHUNK
QT = Q // P
NJOB = B * QT
Y_SCALE = 250000.0
FLOPS = 2 * B * Q * C * K

PT_BUFS = 3
WARM_START = 4
PS_BUFS = 5
HEAD_EV = 3
EV_PER_STEP = {0: 3, 1: 4, 2: 3}
LAST_PREP_STEP = 2
C_ON_V = (6, 7)
HC = C // 2


def tile_guided_cam_module_pa_kernel(tc, x, query, out_0, out_1):
    nc = tc.nc
    xv = x.rearrange("b (g p s) y w -> b g p (s y w)", g=NCH, p=P, s=4)
    qv = query.rearrange("b (h p l) y w -> b p h (l y w)", h=2, p=P, l=2)
    o0v = out_0.rearrange("b (i p l) c -> b i l p c", i=2, p=P, l=2)
    o1v = out_1.rearrange("b (i p l) c -> b i l p c", i=2, p=P, l=2)

    with ExitStack() as ctx:
        ctx.enter_context(tc.manual_schedule())
        const = ctx.enter_context(tc.tile_pool(name="const", bufs=1))
        rawp = ctx.enter_context(tc.tile_pool(name="rawp", bufs=1))
        keep = ctx.enter_context(tc.tile_pool(name="keep", bufs=1))
        stage = ctx.enter_context(tc.tile_pool(name="stage", bufs=4))
        work = ctx.enter_context(tc.tile_pool(name="work", bufs=1))
        small = ctx.enter_context(tc.tile_pool(name="small", bufs=1))
        psum_t = ctx.enter_context(tc.psum_pool(name="psum_t", bufs=PT_BUFS))
        psum_e = ctx.enter_context(tc.psum_pool(name="psum_e", bufs=PS_BUFS))

        halves = [(0, -1, 0)]
        halves.extend([(0, g, h) for g in range(NCH) for h in range(2)])
        halves.append((0, -1, 1))
        halves.extend([(1, c, h) for c in range(-1, NCH) for h in range(2)])

        raw = {}
        for b in range(B):
            for c in range(-1, NCH):
                raw[(b, c)] = rawp.tile([P, 4 * K], BF16, name="raw_%d_%d" % (b, c + 1))

        def load(b, c, h0, h1):
            if c < 0:
                dst = raw[(b, c)][:].rearrange("p (h m) -> p h m", h=2)
                nc.sync.dma_start(out=dst[:, h0:h1, :], in_=qv[b][:, h0:h1, :])
            elif b == 0 and c in (0,):
                for h in range(2):
                    nc.sync.dma_start(out=raw[(b, c)][:, h * 2 * K : (h + 1) * 2 * K], in_=xv[b, c][:, h * 2 * K : (h + 1) * 2 * K])
            else:
                nc.sync.dma_start(out=raw[(b, c)][:], in_=xv[b, c])

        load(0, -1, 0, 1)
        for g in range(NCH):
            load(0, g, 0, 2)
        load(0, -1, 1, 2)
        for c in range(-1, NCH):
            load(1, c, 0, 2)

        zt = const.tile([P, CHUNK], BF16, name="zt")
        nc.vector.memset(zt[:], 0.0)

        def dummy():
            ps = psum_e.tile([P, CHUNK], F32, name="ps", tag="ps")
            nc.tensor.matmul(out=ps[:], lhsT=zt[:, 0:P], rhs=zt[:], start=True, stop=True)

        for k in range(WARM_START):
            dummy()

        ident = const.tile([P, P], F32, name="ident")
        make_identity(nc, ident[:])
        warm = const.tile([P, 2], F32, name="warm")
        nc.vector.memset(warm[:], 0.0)
        nc.scalar.activation(out=warm[:, 1:2], in_=warm[:, 0:1], func=ACT.Exp)

        qc = [keep.tile([P, Q], U32, name="qc%d" % b, align_bytes=64) for b in range(B)]
        qs = [keep.tile([P, Q], U8, name="qs%d" % b, align_bytes=64) for b in range(B)]
        xc = [keep.tile([P, C], U32, name="xc%d" % b, align_bytes=64) for b in range(B)]
        xs = [keep.tile([P, C], U8, name="xs%d" % b, align_bytes=64) for b in range(B)]
        W = [work.tile([P, C], F32, name="W%d" % j) for j in range(NJOB)]
        f8 = [work.tile([P, C], FP8, name="f8_%d" % j) for j in range(NJOB)]
        mins = [small.tile([P, NCH], F32, name="mins%d" % j) for j in range(NJOB)]
        rmin = [small.tile([P, 1], F32, name="rmin%d" % j) for j in range(NJOB)]
        ssum = [small.tile([P, 1], F32, name="ssum%d" % j) for j in range(NJOB)]
        rinv = [small.tile([P, 1], F32, name="rinv%d" % j) for j in range(NJOB)]

        st = {"nt": 0, "ne": 0, "pend": []}

        def tp_next():
            k = st["nt"]
            if k >= len(halves):
                return
            b, c, h = halves[k]
            words = raw[(b, c)][:].bitcast(F32)
            pt = psum_t.tile([P, 4, P], F32, name="pt", tag="pt")
            for l in range(2):
                for u in range(2):
                    s = 2 * h + l
                    nc.tensor.transpose(pt[:, 2 * l + u, :], words[:, s * 256 + u : (s + 1) * 256 : 2], ident[:])
            st[("pt", k)] = pt
            st["nt"] = k + 1

        def ev_next():
            k = st["ne"]
            b, c, h = halves[k]
            alone = b == 0 and c < 0
            if alone or h == 0:
                st[("grp", b, c)] = stage.tile([P, 4 * CHUNK], BF16, name="grp", tag="grp", align_bytes=64)
            grp = st[("grp", b, c)]
            pos = 0 if alone else h
            dst = grp[:].bitcast(F32)[:, 512 * pos : 512 * (pos + 1)].rearrange("k (l p u) -> k l p u", l=2, u=2)
            nc.scalar.copy(out=dst, in_=st[("pt", k)][:].rearrange("k (l u) p -> k l p u", l=2))
            if alone:
                st["pend"].append((b, c, h, 1))
            elif h == 1:
                st["pend"].append((b, c, 0, 2))
            st["ne"] = k + 1

        def flush_q():
            for b, c, h, n in st["pend"]:
                grp = st[("grp", b, c)]
                lo = (0 if c < 0 else c * CHUNK) + h * HALF
                codes, scales = (qc[b], qs[b]) if c < 0 else (xc[b], xs[b])
                nc.vector.quantize_mx(
                    out=codes[:, lo : lo + n * HALF].bitcast(FP8X4),
                    scales=scales[:, lo : lo + n * HALF],
                    in_=grp[:, 0 : n * 4 * HALF],
                )
            st["pend"] = []

        def mm(j, g):
            b, i = divmod(j, QT)
            ps = psum_e.tile([P, CHUNK], F32, name="ps", tag="ps")
            nc.tensor.matmul_mx(
                out=ps[:],
                lhsT=qc[b][:, i * P : (i + 1) * P].bitcast(FP8X4),
                lhsT_scale=qs[b][:, i * P : (i + 1) * P],
                rhs=xc[b][:, g * CHUNK : (g + 1) * CHUNK].bitcast(FP8X4),
                rhs_scale=xs[b][:, g * CHUNK : (g + 1) * CHUNK],
                start=True,
                stop=True,
            )
            st[("ps", j, g)] = ps

        def take(j, g):
            nc.vector.tensor_scalar(
                out=W[j][:, g * CHUNK : (g + 1) * CHUNK].rearrange("q (p s) -> q p s", s=4),
                in0=st[("ps", j, g)][:].rearrange("q (s p) -> q p s", s=4),
                scalar1=1.0,
                scalar2=None,
                op0=ALU.mult,
                op1=ALU.min,
                accum_out=mins[j][:, g : g + 1],
            )

        def rowmin(j):
            nc.vector.tensor_reduce(out=rmin[j][:], in_=mins[j][:], axis=AX.X, op=ALU.min)

        def expo(j):
            nc.scalar.activation(out=W[j][:], in_=W[j][:], func=ACT.Exp, bias=rmin[j][:, 0:1], scale=-1.0, accum_out=ssum[j][:, 0:1])

        def norm(j, order=(0, 1)):
            b, i = divmod(j, QT)
            nc.vector.reciprocal(out=rinv[j][:], in_=ssum[j][:])
            for g in order:
                sl = slice(g * HC, (g + 1) * HC)
                if j in C_ON_V:
                    nc.vector.tensor_scalar(out=W[j][:, sl], in0=W[j][:, sl], scalar1=rinv[j][:, 0:1], scalar2=None, op0=ALU.mult)
                else:
                    nc.gpsimd.tensor_scalar(out=W[j][:, sl], in0=W[j][:, sl], scalar1=rinv[j][:, 0:1], scalar2=0.0, op0=ALU.mult, op1=ALU.add)
                nc.sync.dma_start(out=o0v[b, i // 2, i % 2, :, sl], in_=W[j][:, sl])

        def cast_s(j, lo, hi):
            if hi > lo:
                nc.scalar.activation(out=f8[j][:, lo:hi], in_=W[j][:, lo:hi], func=ACT.Copy, scale=Y_SCALE, saturate=False)

        def cast_v(j, lo, hi):
            nc.vector.tensor_scalar(out=f8[j][:, lo:hi], in0=W[j][:, lo:hi], scalar1=Y_SCALE, scalar2=None, op0=ALU.mult, saturate=False)

        def store_bytes(j, lo, hi):
            b, i = divmod(j, QT)
            if hi > lo:
                nc.sync.dma_start(out=o1v[b, i // 2, i % 2, :, lo:hi], in_=f8[j][:, lo:hi].bitcast(U8))

        for k in range(PT_BUFS):
            tp_next()
            if k % 2 == 0:
                dummy()
        for k in range(2 * NCH + 1):
            ev_next()
            c = halves[k][1]
            full = len(st["pend"]) > 0
            flush_q()
            if full and c >= 1:
                mm(0, c - 1)
                take(0, c - 1)
            if k == 2 * NCH:
                mm(0, NCH - 1)
                take(0, NCH - 1)
            tp_next()
            if k in (1, 3):
                dummy()
        rowmin(0)
        for g in range(NCH):
            mm(1, g)
        for k in range(HEAD_EV):
            ev_next()
        flush_q()

        for j in range(NJOB - 1):
            expo(j)
            for g in range(NCH):
                take(j + 1, g)
            rowmin(j + 1)
            if j >= 1:
                cast_v(j - 1, 0, HC)
                store_bytes(j - 1, 0, HC)
            flush_q()
            while st["nt"] < min(len(halves), st["ne"] + PT_BUFS):
                tp_next()
            if j + 2 < NJOB and j != LAST_PREP_STEP:
                for g in range(NCH):
                    mm(j + 2, g)
            for k in range(EV_PER_STEP.get(j, 0)):
                ev_next()
                tp_next()
            if j == LAST_PREP_STEP:
                flush_q()
                for g in range(NCH):
                    mm(j + 2, g)
            if j in C_ON_V:
                norm(j)
            if j >= 2:
                cast_s(j - 2, HC, C)
                store_bytes(j - 2, HC, C)
            if j not in C_ON_V:
                norm(j)

        last = NJOB - 1
        expo(last)
        cast_v(last - 2, HC, C)
        store_bytes(last - 2, HC, C)
        cast_v(last - 1, 0, C)
        store_bytes(last - 1, 0, C)
        norm(last, (1, 0))
        cast_s(last, HC, C)
        store_bytes(last, HC, C)
        cast_v(last, 0, HC)
        store_bytes(last, 0, HC)
